import numpy as np
import ml_dtypes


def mxq(x, axis, fmt="e4m3"):
    dtype, down = {"e4m3": (ml_dtypes.float8_e4m3fn, 7), "e5m2": (ml_dtypes.float8_e5m2, 14)}[fmt]
    v = np.moveaxis(np.asarray(x, np.float32).astype(ml_dtypes.bfloat16).astype(np.float64), axis, -1)
    blocks = v.reshape(v.shape[:-1] + (-1, 32))
    amax = np.abs(blocks).max(-1, keepdims=True)
    byte = np.maximum(np.where(amax > 0, np.frexp(amax)[1] - 1 + 127, 0) - down, 1)
    scale = np.exp2(byte - 127.0)
    codes = (blocks / scale).astype(np.float32).astype(dtype).astype(np.float64)
    return np.moveaxis((codes * scale).reshape(v.shape), -1, axis)


WIDE = False


def mx_kscale(k):
    if not WIDE:
        return np.ones(k)
    levels = np.array([20, -20, 10, -10, 0])
    a = np.random.permutation(np.resize(levels, k // 512 * 4)).reshape(k // 512, 4)
    idx = np.arange(k)
    return np.exp2(a[idx // 512, idx % 128 // 32])


BF16 = ml_dtypes.bfloat16


def bf(x):
    return np.asarray(x, np.float32).astype(BF16)


def f64(x):
    return np.asarray(x).astype(np.float64)


N, IN, OUT = 512, 4608, 1024
GROUP_MANTISSA = 8
GROUP_SIZE = 36


def on_bfp_grid(x, mantissa=GROUP_MANTISSA, group_size=GROUP_SIZE):
    g = f64(bf(x)).reshape(-1, group_size)
    absmax = np.max(np.abs(g), axis=1, keepdims=True)
    e = np.frexp(np.where(absmax > 0, absmax, 1.0))[1] - 1
    step = np.exp2(e - (mantissa - 1.0))
    q = np.where(absmax > 0, np.trunc(g / step) * step, g)
    return bf(q.reshape(np.shape(x)))


def setup_inputs():
    s = mx_kscale(N)[:, None]
    x = np.random.standard_normal((N, IN)) * s
    w = np.random.uniform(-1.0, 1.0, (OUT, IN)) * 3.0 / np.sqrt(IN)
    b = np.random.uniform(-0.5, 0.5, OUT)
    g = np.random.standard_normal((N, OUT)) * np.exp2(np.random.randint(-12, 1, (N, 1))) / s
    return {"input": on_bfp_grid(x), "weight": on_bfp_grid(w), "bias": bf(b), "grad_out": bf(g)}


def reference(input, weight, bias, grad_out):
    return mxq(f64(grad_out), 0, "e5m2").T @ mxq(f64(input), 0, "e4m3")

@@ -1,0 +1,172 @@
+from contextlib import ExitStack
+
+import concourse.mybir as mybir
+
+BF16 = mybir.dt.bfloat16
+F32 = mybir.dt.float32
+U32 = mybir.dt.uint32
+U8 = mybir.dt.uint8
+E4M3X4 = mybir.dt.float8_e4m3fn_x4
+E5M2X4 = mybir.dt.float8_e5m2_x4
+
+P = 128
+PACK = 4
+TOKENS = P * PACK
+IN = 4608
+OUT = 1024
+CHUNK = 512
+N_CHUNKS = IN // CHUNK
+M_TILES = OUT // P
+HALF = 512
+
+FLOPS = 2 * TOKENS * IN * OUT
+BYTES = TOKENS * IN * 2 + TOKENS * OUT * 2 + OUT * IN * 4
+
+PINNED = True
+GROUPS = ((0, 4), (4, 9))
+X_LOADS = ((0, 2), (2, 4), (4, 9))
+
+
+def tile_bflinear_kernel(tc, x, weight, bias, grad_out, out):
+    nc = tc.nc
+    with ExitStack() as ctx:
+        if PINNED:
+            ctx.enter_context(tc.manual_schedule())
+        keep = ctx.enter_context(tc.tile_pool(name="keep", bufs=1))
+        stage = ctx.enter_context(tc.tile_pool(name="stage", bufs=8))
+        psum = ctx.enter_context(tc.psum_pool(name="psum", bufs=8))
+
+        g_raw = [keep.tile([P, PACK, HALF], BF16, name="g_raw%d" % h) for h in range(2)]
+        g_grp = [keep.tile([P, HALF, PACK], BF16, name="g_grp%d" % h, align_bytes=64) for h in range(2)]
+        g_codes = [keep.tile([P, HALF], U32, name="g_codes%d" % h, align_bytes=64) for h in range(2)]
+        g_scales = [keep.tile([P, HALF], U8, name="g_scales%d" % h, align_bytes=64) for h in range(2)]
+        x_raw = [
+            keep.tile([P, PACK, (b - a) * CHUNK], BF16, name="x_raw%d" % i) for i, (a, b) in enumerate(X_LOADS)
+        ]
+        x_grp = [keep.tile([P, CHUNK, PACK], BF16, name="x_grp%d" % c, align_bytes=64) for c in range(N_CHUNKS)]
+        x_codes = [keep.tile([P, CHUNK], U32, name="x_codes%d" % c, align_bytes=64) for c in range(N_CHUNKS)]
+        x_scales = [keep.tile([P, CHUNK], U8, name="x_scales%d" % c, align_bytes=64) for c in range(N_CHUNKS)]
+
+        def load_g(h):
+            nc.sync.dma_start(
+                out=g_raw[h][:],
+                in_=grad_out[:, h * HALF : (h + 1) * HALF].rearrange("(p j) w -> p j w", j=PACK),
+            )
+
+        def load_x(i):
+            a, b = X_LOADS[i]
+            nc.sync.dma_start(
+                out=x_raw[i][:],
+                in_=x[:, a * CHUNK : b * CHUNK].rearrange("(p j) w -> p j w", j=PACK),
+            )
+
+        def regroup(copy, grouped, raw):
+            copy(
+                out=grouped.rearrange("p (c i) t -> p c t i", i=4),
+                in_=raw.rearrange("p t (c i) -> p c t i", i=4),
+            )
+
+        def regroup_g(copy, h):
+            regroup(copy, g_grp[h][:], g_raw[h][:])
+
+        def regroup_x(copy, c):
+            for i, (a, b) in enumerate(X_LOADS):
+                if a <= c < b:
+                    regroup(copy, x_grp[c][:], x_raw[i][:, :, (c - a) * CHUNK : (c - a + 1) * CHUNK])
+
+        def quantise_g(h):
+            nc.vector.quantize_mx(
+                out=g_codes[h][:].bitcast(E5M2X4),
+                scales=g_scales[h][:],
+                in_=g_grp[h][:].rearrange("p w t -> p (w t)"),
+            )
+
+        def quantise_x(c):
+            nc.vector.quantize_mx(
+                out=x_codes[c][:].bitcast(E4M3X4),
+                scales=x_scales[c][:],
+                in_=x_grp[c][:].rearrange("p w t -> p (w t)"),
+            )
+
+        V = nc.vector.tensor_copy
+        S = nc.scalar.copy
+
+        def product(m, g, engines):
+            a, b = GROUPS[g]
+            h, mm = divmod(m, M_TILES // 2)
+            cols = slice(mm * P, (mm + 1) * P)
+            st = stage.tile([P, (b - a) * CHUNK], F32, name="st", tag="st")
+            accs = []
+            for c in range(a, b):
+                acc = psum.tile([P, CHUNK], F32, name="acc", tag="acc")
+                nc.tensor.matmul_mx(
+                    out=acc[:],
+                    lhsT=g_codes[h][:, cols].bitcast(E5M2X4),
+                    lhsT_scale=g_scales[h][:, cols],
+                    rhs=x_codes[c][:].bitcast(E4M3X4),
+                    rhs_scale=x_scales[c][:],
+                    start=True,
+                    stop=True,
+                )
+                accs.append(acc)
+            return st, accs
+
+        def evacuate(copy, prod, g, c):
+            st, accs = prod
+            a, b = GROUPS[g]
+            copy(out=st[:, (c - a) * CHUNK : (c - a + 1) * CHUNK], in_=accs[c - a][:])
+
+        def store(prod, m, g):
+            a, b = GROUPS[g]
+            nc.sync.dma_start(out=out[m * P : (m + 1) * P, a * CHUNK : b * CHUNK], in_=prod[0][:])
+
+        load_g(0)
+        load_x(0)
+        load_x(1)
+        load_g(1)
+        load_x(2)
+
+        regroup_g(V, 0)
+        quantise_g(0)
+        regroup_x(V, 0)
+        regroup_x(S, 1)
+        quantise_x(0)
+        quantise_x(1)
+        regroup_x(V, 2)
+        regroup_x(S, 3)
+        quantise_x(2)
+        quantise_x(3)
+
+        for m in range(4):
+            prod = product(m, 0, None)
+            for c in range(3):
+                evacuate(S, prod, 0, c)
+            evacuate(V, prod, 0, 3)
+            store(prod, m, 0)
+            if m == 0:
+                regroup_g(V, 1)
+            if m == 1:
+                quantise_g(1)
+
+        regroup_x(V, 4)
+        regroup_x(V, 5)
+        quantise_x(4)
+        regroup_x(V, 6)
+        quantise_x(5)
+        regroup_x(V, 7)
+        quantise_x(6)
+        regroup_x(V, 8)
+        quantise_x(7)
+        quantise_x(8)
+        for m in range(4, M_TILES):
+            prod = product(m, 0, None)
+            for c in range(4):
+                evacuate(S, prod, 0, c)
+            store(prod, m, 0)
+
+        for m in range(M_TILES):
+            prod = product(m, 1, None)
+            n_scalar = 3 if m % 2 == 0 else 2
+            for c in range(4, 9):
+                evacuate(S if c - 4 < n_scalar else V, prod, 1, c)
+            store(prod, m, 1)

@@ -22,7 +22,7 @@ HALF = 512
 FLOPS = 2 * TOKENS * IN * OUT
 BYTES = TOKENS * IN * 2 + TOKENS * OUT * 2 + OUT * IN * 4
 
-PINNED = True
+PINNED = False
 GROUPS = ((0, 4), (4, 9))
 X_LOADS = ((0, 2), (2, 4), (4, 9))
 

@@ -22,8 +22,8 @@ HALF = 512
 FLOPS = 2 * TOKENS * IN * OUT
 BYTES = TOKENS * IN * 2 + TOKENS * OUT * 2 + OUT * IN * 4
 
-PINNED = False
-GROUPS = ((0, 4), (4, 9))
+PINNED = True
+FIRST = (3, 3, 3, 3, 4, 4, 4, 4)
 X_LOADS = ((0, 2), (2, 4), (4, 9))
 
 
@@ -91,8 +91,7 @@ def tile_bflinear_kernel(tc, x, weight, bias, grad_out, out):
         V = nc.vector.tensor_copy
         S = nc.scalar.copy
 
-        def product(m, g, engines):
-            a, b = GROUPS[g]
+        def product(m, a, b):
             h, mm = divmod(m, M_TILES // 2)
             cols = slice(mm * P, (mm + 1) * P)
             st = stage.tile([P, (b - a) * CHUNK], F32, name="st", tag="st")
@@ -109,16 +108,15 @@ def tile_bflinear_kernel(tc, x, weight, bias, grad_out, out):
                     stop=True,
                 )
                 accs.append(acc)
-            return st, accs
+            return st, accs, a, b
 
-        def evacuate(copy, prod, g, c):
-            st, accs = prod
-            a, b = GROUPS[g]
+        def evacuate(copy, prod, c):
+            st, accs, a, b = prod
             copy(out=st[:, (c - a) * CHUNK : (c - a + 1) * CHUNK], in_=accs[c - a][:])
 
-        def store(prod, m, g):
-            a, b = GROUPS[g]
-            nc.sync.dma_start(out=out[m * P : (m + 1) * P, a * CHUNK : b * CHUNK], in_=prod[0][:])
+        def store(prod, m):
+            st, accs, a, b = prod
+            nc.sync.dma_start(out=out[m * P : (m + 1) * P, a * CHUNK : b * CHUNK], in_=st[:])
 
         load_g(0)
         load_x(0)
@@ -138,11 +136,11 @@ def tile_bflinear_kernel(tc, x, weight, bias, grad_out, out):
         quantise_x(3)
 
         for m in range(4):
-            prod = product(m, 0, None)
-            for c in range(3):
-                evacuate(S, prod, 0, c)
-            evacuate(V, prod, 0, 3)
-            store(prod, m, 0)
+            prod = product(m, 0, FIRST[m])
+            for c in range(FIRST[m] - 1):
+                evacuate(S, prod, c)
+            evacuate(V, prod, FIRST[m] - 1)
+            store(prod, m)
             if m == 0:
                 regroup_g(V, 1)
             if m == 1:
@@ -159,14 +157,15 @@ def tile_bflinear_kernel(tc, x, weight, bias, grad_out, out):
         quantise_x(7)
         quantise_x(8)
         for m in range(4, M_TILES):
-            prod = product(m, 0, None)
-            for c in range(4):
-                evacuate(S, prod, 0, c)
-            store(prod, m, 0)
+            prod = product(m, 0, FIRST[m])
+            for c in range(FIRST[m]):
+                evacuate(S, prod, c)
+            store(prod, m)
 
+        turn = 0
         for m in range(M_TILES):
-            prod = product(m, 1, None)
-            n_scalar = 3 if m % 2 == 0 else 2
-            for c in range(4, 9):
-                evacuate(S if c - 4 < n_scalar else V, prod, 1, c)
-            store(prod, m, 1)
+            prod = product(m, FIRST[m], N_CHUNKS)
+            for c in range(FIRST[m], N_CHUNKS):
+                evacuate(S if turn % 2 == 0 else V, prod, c)
+                turn += 1
+            store(prod, m)

@@ -36,12 +36,12 @@ def tile_bflinear_kernel(tc, x, weight, bias, grad_out, out):
         stage = ctx.enter_context(tc.tile_pool(name="stage", bufs=8))
         psum = ctx.enter_context(tc.psum_pool(name="psum", bufs=8))
 
-        g_raw = [keep.tile([P, PACK, HALF], BF16, name="g_raw%d" % h) for h in range(2)]
+        g_raw = [keep.tile([P, PACK, HALF], BF16, name="g_raw%d" % h, align_bytes=256) for h in range(2)]
         g_grp = [keep.tile([P, HALF, PACK], BF16, name="g_grp%d" % h, align_bytes=64) for h in range(2)]
         g_codes = [keep.tile([P, HALF], U32, name="g_codes%d" % h, align_bytes=64) for h in range(2)]
         g_scales = [keep.tile([P, HALF], U8, name="g_scales%d" % h, align_bytes=64) for h in range(2)]
         x_raw = [
-            keep.tile([P, PACK, (b - a) * CHUNK], BF16, name="x_raw%d" % i) for i, (a, b) in enumerate(X_LOADS)
+            keep.tile([P, PACK, (b - a) * CHUNK], BF16, name="x_raw%d" % i, align_bytes=256) for i, (a, b) in enumerate(X_LOADS)
         ]
         x_grp = [keep.tile([P, CHUNK, PACK], BF16, name="x_grp%d" % c, align_bytes=64) for c in range(N_CHUNKS)]
         x_codes = [keep.tile([P, CHUNK], U32, name="x_codes%d" % c, align_bytes=64) for c in range(N_CHUNKS)]
@@ -94,7 +94,7 @@ def tile_bflinear_kernel(tc, x, weight, bias, grad_out, out):
         def product(m, a, b):
             h, mm = divmod(m, M_TILES // 2)
             cols = slice(mm * P, (mm + 1) * P)
-            st = stage.tile([P, (b - a) * CHUNK], F32, name="st", tag="st")
+            st = stage.tile([P, (b - a) * CHUNK], F32, name="st", tag="st", align_bytes=256)
             accs = []
             for c in range(a, b):
                 acc = psum.tile([P, CHUNK], F32, name="acc", tag="acc")

@@ -36,13 +36,13 @@ def tile_bflinear_kernel(tc, x, weight, bias, grad_out, out):
         stage = ctx.enter_context(tc.tile_pool(name="stage", bufs=8))
         psum = ctx.enter_context(tc.psum_pool(name="psum", bufs=8))
 
-        g_raw = [keep.tile([P, PACK, HALF], BF16, name="g_raw%d" % h, align_bytes=256) for h in range(2)]
+        g_raw = [keep.tile([P, PACK, HALF], BF16, name="g_raw%d" % h, align_bytes=4096) for h in range(2)]
+        x_raw = [
+            keep.tile([P, PACK, (b - a) * CHUNK], BF16, name="x_raw%d" % i, align_bytes=4096) for i, (a, b) in enumerate(X_LOADS)
+        ]
         g_grp = [keep.tile([P, HALF, PACK], BF16, name="g_grp%d" % h, align_bytes=64) for h in range(2)]
         g_codes = [keep.tile([P, HALF], U32, name="g_codes%d" % h, align_bytes=64) for h in range(2)]
         g_scales = [keep.tile([P, HALF], U8, name="g_scales%d" % h, align_bytes=64) for h in range(2)]
-        x_raw = [
-            keep.tile([P, PACK, (b - a) * CHUNK], BF16, name="x_raw%d" % i, align_bytes=256) for i, (a, b) in enumerate(X_LOADS)
-        ]
         x_grp = [keep.tile([P, CHUNK, PACK], BF16, name="x_grp%d" % c, align_bytes=64) for c in range(N_CHUNKS)]
         x_codes = [keep.tile([P, CHUNK], U32, name="x_codes%d" % c, align_bytes=64) for c in range(N_CHUNKS)]
         x_scales = [keep.tile([P, CHUNK], U8, name="x_scales%d" % c, align_bytes=64) for c in range(N_CHUNKS)]
@@ -94,7 +94,7 @@ def tile_bflinear_kernel(tc, x, weight, bias, grad_out, out):
         def product(m, a, b):
             h, mm = divmod(m, M_TILES // 2)
             cols = slice(mm * P, (mm + 1) * P)
-            st = stage.tile([P, (b - a) * CHUNK], F32, name="st", tag="st", align_bytes=256)
+            st = stage.tile([P, (b - a) * CHUNK], F32, name="st", tag="st", align_bytes=4096)
             accs = []
             for c in range(a, b):
                 acc = psum.tile([P, CHUNK], F32, name="acc", tag="acc")

@@ -32,8 +32,8 @@ def tile_bflinear_kernel(tc, x, weight, bias, grad_out, out):
     with ExitStack() as ctx:
         if PINNED:
             ctx.enter_context(tc.manual_schedule())
-        keep = ctx.enter_context(tc.tile_pool(name="keep", bufs=1))
         stage = ctx.enter_context(tc.tile_pool(name="stage", bufs=8))
+        keep = ctx.enter_context(tc.tile_pool(name="keep", bufs=1))
         psum = ctx.enter_context(tc.psum_pool(name="psum", bufs=8))
 
         g_raw = [keep.tile([P, PACK, HALF], BF16, name="g_raw%d" % h, align_bytes=4096) for h in range(2)]

from contextlib import ExitStack

import concourse.mybir as mybir

BF16 = mybir.dt.bfloat16
F32 = mybir.dt.float32
U32 = mybir.dt.uint32
U8 = mybir.dt.uint8
E4M3X4 = mybir.dt.float8_e4m3fn_x4
E5M2X4 = mybir.dt.float8_e5m2_x4

P = 128
PACK = 4
TOKENS = P * PACK
IN = 4608
OUT = 1024
CHUNK = 512
N_CHUNKS = IN // CHUNK
M_TILES = OUT // P
HALF = 512

FLOPS = 2 * TOKENS * IN * OUT
BYTES = TOKENS * IN * 2 + TOKENS * OUT * 2 + OUT * IN * 4

PINNED = True
FIRST = (3, 3, 3, 3, 4, 4, 4, 4)
X_LOADS = ((0, 2), (2, 4), (4, 9))


def tile_bflinear_kernel(tc, x, weight, bias, grad_out, out):
    nc = tc.nc
    with ExitStack() as ctx:
        if PINNED:
            ctx.enter_context(tc.manual_schedule())
        stage = ctx.enter_context(tc.tile_pool(name="stage", bufs=8))
        keep = ctx.enter_context(tc.tile_pool(name="keep", bufs=1))
        psum = ctx.enter_context(tc.psum_pool(name="psum", bufs=8))

        g_raw = [keep.tile([P, PACK, HALF], BF16, name="g_raw%d" % h, align_bytes=4096) for h in range(2)]
        x_raw = [
            keep.tile([P, PACK, (b - a) * CHUNK], BF16, name="x_raw%d" % i, align_bytes=4096) for i, (a, b) in enumerate(X_LOADS)
        ]
        g_grp = [keep.tile([P, HALF, PACK], BF16, name="g_grp%d" % h, align_bytes=64) for h in range(2)]
        g_codes = [keep.tile([P, HALF], U32, name="g_codes%d" % h, align_bytes=64) for h in range(2)]
        g_scales = [keep.tile([P, HALF], U8, name="g_scales%d" % h, align_bytes=64) for h in range(2)]
        x_grp = [keep.tile([P, CHUNK, PACK], BF16, name="x_grp%d" % c, align_bytes=64) for c in range(N_CHUNKS)]
        x_codes = [keep.tile([P, CHUNK], U32, name="x_codes%d" % c, align_bytes=64) for c in range(N_CHUNKS)]
        x_scales = [keep.tile([P, CHUNK], U8, name="x_scales%d" % c, align_bytes=64) for c in range(N_CHUNKS)]

        def load_g(h):
            nc.sync.dma_start(
                out=g_raw[h][:],
                in_=grad_out[:, h * HALF : (h + 1) * HALF].rearrange("(p j) w -> p j w", j=PACK),
            )

        def load_x(i):
            a, b = X_LOADS[i]
            nc.sync.dma_start(
                out=x_raw[i][:],
                in_=x[:, a * CHUNK : b * CHUNK].rearrange("(p j) w -> p j w", j=PACK),
            )

        def regroup(copy, grouped, raw):
            copy(
                out=grouped.rearrange("p (c i) t -> p c t i", i=4),
                in_=raw.rearrange("p t (c i) -> p c t i", i=4),
            )

        def regroup_g(copy, h):
            regroup(copy, g_grp[h][:], g_raw[h][:])

        def regroup_x(copy, c):
            for i, (a, b) in enumerate(X_LOADS):
                if a <= c < b:
                    regroup(copy, x_grp[c][:], x_raw[i][:, :, (c - a) * CHUNK : (c - a + 1) * CHUNK])

        def quantise_g(h):
            nc.vector.quantize_mx(
                out=g_codes[h][:].bitcast(E5M2X4),
                scales=g_scales[h][:],
                in_=g_grp[h][:].rearrange("p w t -> p (w t)"),
            )

        def quantise_x(c):
            nc.vector.quantize_mx(
                out=x_codes[c][:].bitcast(E4M3X4),
                scales=x_scales[c][:],
                in_=x_grp[c][:].rearrange("p w t -> p (w t)"),
            )

        V = nc.vector.tensor_copy
        S = nc.scalar.copy

        def product(m, a, b):
            h, mm = divmod(m, M_TILES // 2)
            cols = slice(mm * P, (mm + 1) * P)
            st = stage.tile([P, (b - a) * CHUNK], F32, name="st", tag="st", align_bytes=4096)
            accs = []
            for c in range(a, b):
                acc = psum.tile([P, CHUNK], F32, name="acc", tag="acc")
                nc.tensor.matmul_mx(
                    out=acc[:],
                    lhsT=g_codes[h][:, cols].bitcast(E5M2X4),
                    lhsT_scale=g_scales[h][:, cols],
                    rhs=x_codes[c][:].bitcast(E4M3X4),
                    rhs_scale=x_scales[c][:],
                    start=True,
                    stop=True,
                )
                accs.append(acc)
            return st, accs, a, b

        def evacuate(copy, prod, c):
            st, accs, a, b = prod
            copy(out=st[:, (c - a) * CHUNK : (c - a + 1) * CHUNK], in_=accs[c - a][:])

        def store(prod, m):
            st, accs, a, b = prod
            nc.sync.dma_start(out=out[m * P : (m + 1) * P, a * CHUNK : b * CHUNK], in_=st[:])

        load_g(0)
        load_x(0)
        load_x(1)
        load_g(1)
        load_x(2)

        regroup_g(V, 0)
        quantise_g(0)
        regroup_x(V, 0)
        regroup_x(S, 1)
        quantise_x(0)
        quantise_x(1)
        regroup_x(V, 2)
        regroup_x(S, 3)
        quantise_x(2)
        quantise_x(3)

        for m in range(4):
            prod = product(m, 0, FIRST[m])
            for c in range(FIRST[m] - 1):
                evacuate(S, prod, c)
            evacuate(V, prod, FIRST[m] - 1)
            store(prod, m)
            if m == 0:
                regroup_g(V, 1)
            if m == 1:
                quantise_g(1)

        regroup_x(V, 4)
        regroup_x(V, 5)
        quantise_x(4)
        regroup_x(V, 6)
        quantise_x(5)
        regroup_x(V, 7)
        quantise_x(6)
        regroup_x(V, 8)
        quantise_x(7)
        quantise_x(8)
        for m in range(4, M_TILES):
            prod = product(m, 0, FIRST[m])
            for c in range(FIRST[m]):
                evacuate(S, prod, c)
            store(prod, m)

        turn = 0
        for m in range(M_TILES):
            prod = product(m, FIRST[m], N_CHUNKS)
            for c in range(FIRST[m], N_CHUNKS):
                evacuate(S if turn % 2 == 0 else V, prod, c)
                turn += 1
            store(prod, m)
